import numpy as np
import ml_dtypes


def mxq(x, axis, fmt="e4m3"):
    dtype, down = {"e4m3": (ml_dtypes.float8_e4m3fn, 7), "e5m2": (ml_dtypes.float8_e5m2, 14)}[fmt]
    v = np.moveaxis(np.asarray(x, np.float32).astype(ml_dtypes.bfloat16).astype(np.float64), axis, -1)
    blocks = v.reshape(v.shape[:-1] + (-1, 32))
    amax = np.abs(blocks).max(-1, keepdims=True)
    byte = np.maximum(np.where(amax > 0, np.frexp(amax)[1] - 1 + 127, 0) - down, 1)
    scale = np.exp2(byte - 127.0)
    codes = (blocks / scale).astype(np.float32).astype(dtype).astype(np.float64)
    return np.moveaxis((codes * scale).reshape(v.shape), -1, axis)


WIDE = False


def mx_kscale(k):
    if not WIDE:
        return np.ones(k)
    levels = np.array([10, -10, 5, -5, 0])
    a = np.random.permutation(np.resize(levels, k // 512 * 4)).reshape(k // 512, 4)
    idx = np.arange(k)
    return np.exp2(a[idx // 512, idx % 128 // 32])


BF16 = ml_dtypes.bfloat16


def bf(x):
    return np.asarray(x, np.float32).astype(BF16)


def f64(x):
    return np.asarray(x).astype(np.float64)


B, OBS, ACT, U, KSUB = 1024, 383, 128, 1024, 2
DT = 1.0 / KSUB
LN_EPS = 1e-5


def mish(v):
    return v * np.tanh(np.log(1.0 + np.exp(v)))


def layer_norm(v, g, b):
    mu = v.mean(-1, keepdims=True)
    var = np.square(v - mu).mean(-1, keepdims=True)
    return (v - mu) / np.sqrt(var + LN_EPS) * g + b


def setup_inputs():
    s, t = mx_kscale(U), mx_kscale(U)
    return {"h0": bf(np.random.standard_normal((B, U)) * s),
            "z": bf(np.random.standard_normal((B, ACT)) * 0.5),
            "k1": bf(np.random.standard_normal((B, ACT))),
            "W1": bf(np.random.standard_normal((U, U)) / np.sqrt(U) / s[:, None]),
            "b1": bf(np.random.standard_normal(U) * 0.3),
            "ln1_g": bf((1.0 + 0.1 * np.random.standard_normal(U)) * t),
            "ln1_b": bf(0.1 * np.random.standard_normal(U) * t),
            "W2": bf(np.random.standard_normal((U, ACT)) / np.sqrt(U) / t[:, None]),
            "b2": bf(np.random.standard_normal(ACT) * 0.3)}


def reference(h0, z, k1, W1, b1, ln1_g, ln1_b, W2, b2):
    h1 = layer_norm(mish((mxq(f64(h0), 1, "e4m3") @ mxq(f64(W1), 0, "e4m3")) + f64(b1)), f64(ln1_g), f64(ln1_b))
    k2 = (mxq(h1, 1, "e4m3") @ mxq(f64(W2), 0, "e4m3")) + f64(b2)
    return f64(z) + (DT / 2.0) * (f64(k1) + k2)

@@ -1,0 +1,351 @@
+from contextlib import ExitStack
+
+import concourse.mybir as mybir
+from concourse.masks import make_identity
+
+F32 = mybir.dt.float32
+BF16 = mybir.dt.bfloat16
+U32 = mybir.dt.uint32
+U8 = mybir.dt.uint8
+FP8X4 = mybir.dt.float8_e4m3fn_x4
+FUNC = mybir.ActivationFunctionType
+ALU = mybir.AluOpType
+
+P = 128
+PACK = 4
+K_PASS = P * PACK
+BATCH, UNITS, ACTIONS = 1024, 1024, 128
+TILES = BATCH // P
+PASSES = UNITS // K_PASS
+BANK = 512
+HALVES = UNITS // BANK
+BLOCKS = UNITS // P
+LN_EPS = 1e-5
+ROOT_UNITS = 32.0
+QUARTER = 0.25
+SMALLEST = 2.0 ** -60
+TILES_PER_BATCH = BANK // P
+
+FLOPS = 2 * BATCH * UNITS * UNITS + 2 * BATCH * UNITS * ACTIONS
+
+
+def tile_actorflowode_pb_kernel(tc, h0, z, k1, W1, b1, ln1_g, ln1_b, W2, b2, out):
+    nc = tc.nc
+    with ExitStack() as ctx:
+        keep = ctx.enter_context(tc.tile_pool(name="keep", bufs=1))
+        stage = ctx.enter_context(tc.tile_pool(name="stage", bufs=2))
+        psum = ctx.enter_context(tc.psum_pool(name="psum", bufs=8))
+        ctx.enter_context(tc.manual_schedule())
+
+        smallest = keep.tile([P, 1], F32)
+        nc.vector.memset(smallest[:], SMALLEST)
+        neg_half = keep.tile([P, 1], F32)
+        nc.vector.memset(neg_half[:], -0.5)
+        ones = keep.tile([P, P], BF16)
+        nc.vector.memset(ones[:], 1.0)
+        bias_rows = keep.tile([P, UNITS + 2 * ACTIONS], BF16)
+        nc.vector.memset(bias_rows[:], 0.0)
+        norm_rows = keep.tile([P, P], BF16)
+        nc.vector.memset(norm_rows[:], 0.0)
+        ident_f32 = keep.tile([P, P], F32)
+        make_identity(nc, ident_f32[:])
+        ident_bf16 = keep.tile([P, P], BF16)
+        make_identity(nc, ident_bf16[:])
+
+        nc.scalar.dma_start(out=bias_rows[0:1, 0:UNITS], in_=b1.rearrange("(o n) -> o n", o=1))
+        nc.scalar.dma_start(
+            out=bias_rows[0:1, UNITS : UNITS + ACTIONS], in_=b2.rearrange("(o n) -> o n", o=1)
+        )
+        nc.scalar.dma_start(out=norm_rows[0:BLOCKS, :], in_=ln1_g.rearrange("(j p) -> j p", p=P))
+        nc.scalar.dma_start(
+            out=norm_rows[BLOCKS : 2 * BLOCKS, :], in_=ln1_b.rearrange("(j p) -> j p", p=P)
+        )
+
+        warm = keep.tile([P, 1], F32)
+        nc.scalar.activation(out=warm[:], in_=smallest[:], func=FUNC.Sigmoid)
+
+        w1_raw = keep.tile([P, PASSES, PACK, UNITS], BF16)
+
+        def load_w1(half, g):
+            cols = slice(BANK * half, BANK * (half + 1))
+            for u in range(2):
+                first = K_PASS * g + 2 * P * u
+                nc.sync.dma_start(
+                    out=w1_raw[:, g, 2 * u : 2 * u + 2, cols],
+                    in_=W1[first : first + 2 * P, cols].rearrange("(p e) n -> p e n", e=2),
+                )
+
+        h0_raw = [keep.tile([P, UNITS], BF16, name="h0_raw%d" % i) for i in range(TILES)]
+
+        def load_h0(i):
+            nc.sync.dma_start(out=h0_raw[i][:], in_=h0[P * i : P * (i + 1), :])
+
+        for half in range(HALVES):
+            for g in range(PASSES):
+                load_w1(half, g)
+        for i in range(TILES):
+            load_h0(i)
+        w2_raw = keep.tile([P, BLOCKS, ACTIONS], BF16)
+        nc.sync.dma_start(out=w2_raw[:], in_=W2.rearrange("(j p) a -> p j a", p=P))
+        z_rows = keep.tile([P, TILES, ACTIONS], BF16)
+        nc.sync.dma_start(out=z_rows[:], in_=z.rearrange("(i p) a -> p i a", p=P))
+        k1_rows = keep.tile([P, TILES, ACTIONS], BF16)
+        nc.sync.dma_start(out=k1_rows[:], in_=k1.rearrange("(i p) a -> p i a", p=P))
+
+        bias1 = keep.tile([P, UNITS], BF16)
+        for half in range(HALVES):
+            cols = slice(BANK * half, BANK * (half + 1))
+            spread = psum.tile([P, BANK], F32, tag="bank")
+            nc.tensor.matmul(out=spread[:], lhsT=ones[:], rhs=bias_rows[:, cols], start=True, stop=True)
+            nc.scalar.copy(out=bias1[:, cols], in_=spread[:])
+        bias2 = keep.tile([P, ACTIONS], F32)
+        spread = psum.tile([P, 2 * ACTIONS], F32, tag="bank")
+        nc.tensor.matmul(out=spread[:], lhsT=ones[:], rhs=bias_rows[:, UNITS:], start=True, stop=True)
+        nc.scalar.copy(out=bias2[:], in_=spread[:, 0:ACTIONS])
+        norm_cols = psum.tile([P, P], BF16, tag="bank")
+        nc.tensor.transpose(norm_cols[:], norm_rows[:], ident_bf16[:])
+        gain = keep.tile([P, BLOCKS], F32)
+        nc.scalar.mul(out=gain[:], in_=norm_cols[:, 0:BLOCKS], mul=ROOT_UNITS)
+        shift = keep.tile([P, BLOCKS], F32)
+        nc.scalar.copy(out=shift[:], in_=norm_cols[:, BLOCKS : 2 * BLOCKS])
+
+        w1_codes = keep.tile([P, PASSES, UNITS], U32, align_bytes=64)
+        w1_scales = keep.tile([P, PASSES, UNITS], U8, align_bytes=64)
+        w1_grouped = {}
+
+        def regroup_w1(half, g):
+            cols = slice(BANK * half, BANK * (half + 1))
+            grouped = keep.tile([P, BANK, PACK], BF16, align_bytes=64, name="w1_grouped%d%d" % (half, g))
+            nc.vector.tensor_copy(
+                out=grouped[:].rearrange("p (c i) t -> p c t i", i=4),
+                in_=w1_raw[:, g, :, cols].rearrange("p t (c i) -> p c t i", i=4),
+            )
+            w1_grouped[(half, g)] = grouped
+
+        def quantise_w1(half, g):
+            cols = slice(BANK * half, BANK * (half + 1))
+            nc.vector.quantize_mx(
+                out=w1_codes[:, g, cols].bitcast(FP8X4),
+                scales=w1_scales[:, g, cols],
+                in_=w1_grouped[(half, g)][:].rearrange("p n t -> p (n t)"),
+            )
+
+        regroup_w1(0, 0)
+        regroup_w1(0, 1)
+        quantise_w1(0, 0)
+        regroup_w1(1, 0)
+        quantise_w1(0, 1)
+        regroup_w1(1, 1)
+        quantise_w1(1, 0)
+        quantise_w1(1, 1)
+
+        h0_codes = keep.tile([P, TILES, PASSES * P], U32, align_bytes=64)
+        h0_scales = keep.tile([P, TILES, PASSES * P], U8, align_bytes=64)
+        h0_grouped = [
+            keep.tile([P, UNITS], BF16, align_bytes=64, name="h0_grouped%d" % i) for i in range(TILES)
+        ]
+        pre = [keep.tile([P, UNITS], F32, name="pre%d" % i) for i in range(TILES)]
+        work = [keep.tile([P, UNITS], F32, name="work%d" % i) for i in range(TILES)]
+
+        def transpose_h0(i, copy):
+            words = h0_raw[i][:].bitcast(F32)
+            flipped = psum.tile([P, PACK, P], F32, tag="bank")
+            for j in range(PACK):
+                nc.tensor.transpose(flipped[:, j, :], words[:, P * j : P * (j + 1)], ident_f32[:])
+            copy(
+                out=h0_grouped[i][:].bitcast(F32).rearrange("p (g b u) -> p g b u", g=PASSES, u=2),
+                in_=flipped[:].rearrange("p (g u) b -> p g b u", u=2),
+            )
+
+        def quantise_h0(i):
+            nc.vector.quantize_mx(
+                out=h0_codes[:, i, :].bitcast(FP8X4), scales=h0_scales[:, i, :], in_=h0_grouped[i][:]
+            )
+
+        def first_product(i):
+            for half in range(HALVES):
+                cols = slice(BANK * half, BANK * (half + 1))
+                acc = psum.tile([P, BANK], F32, tag="bank")
+                for g in range(PASSES):
+                    rows = slice(P * g, P * (g + 1))
+                    nc.tensor.matmul_mx(
+                        out=acc[:],
+                        lhsT=h0_codes[:, i, rows].bitcast(FP8X4),
+                        lhsT_scale=h0_scales[:, i, rows],
+                        rhs=w1_codes[:, g, cols].bitcast(FP8X4),
+                        rhs_scale=w1_scales[:, g, cols],
+                        start=(g == 0),
+                        stop=(g == PASSES - 1),
+                    )
+                nc.vector.tensor_tensor(out=pre[i][:, cols], in0=acc[:], in1=bias1[:, cols], op=ALU.add)
+
+        def prepare(batch, copy):
+            for i in batch:
+                transpose_h0(i, copy)
+            for i in batch:
+                quantise_h0(i)
+            for i in batch:
+                first_product(i)
+
+        def sigmoid(i):
+            nc.scalar.activation(out=work[i][:], in_=pre[i][:], func=FUNC.Sigmoid, scale=-1.0)
+
+        def log(i):
+            nc.scalar.activation(out=work[i][:], in_=work[i][:], func=FUNC.Ln, bias=smallest[:])
+
+        def tanh(i):
+            nc.scalar.activation(out=work[i][:], in_=work[i][:], func=FUNC.Tanh, scale=-1.0)
+
+        total = [keep.tile([P, 1], F32, name="total%d" % i) for i in range(TILES)]
+        neg_mean = [keep.tile([P, 1], F32, name="neg_mean%d" % i) for i in range(TILES)]
+        squares = [keep.tile([P, 1], F32, name="squares%d" % i) for i in range(TILES)]
+        padded = [keep.tile([P, 1], F32, name="padded%d" % i) for i in range(TILES)]
+        inv_std = [keep.tile([P, 1], F32, name="inv_std%d" % i) for i in range(TILES)]
+
+        def mish(i):
+            nc.vector.scalar_tensor_tensor(
+                out=pre[i][:], in0=pre[i][:], scalar=1.0, in1=work[i][:],
+                op0=ALU.mult, op1=ALU.mult, accum_out=total[i][:],
+            )
+            nc.gpsimd.tensor_scalar(
+                out=neg_mean[i][:], in0=total[i][:], scalar1=-1.0 / UNITS, scalar2=0.0,
+                op0=ALU.mult, op1=ALU.add,
+            )
+
+        def variance(i):
+            nc.scalar.activation(
+                out=work[i][:], in_=pre[i][:], func=FUNC.Square, bias=neg_mean[i][:],
+                accum_out=squares[i][:],
+            )
+            nc.gpsimd.tensor_scalar(
+                out=padded[i][:], in0=squares[i][:], scalar1=1.0, scalar2=UNITS * LN_EPS,
+                op0=ALU.mult, op1=ALU.add,
+            )
+            nc.gpsimd.tensor_tensor(out=inv_std[i][:], in0=padded[i][:], in1=neg_half[:], op=ALU.pow)
+
+        def normalise(i):
+            nc.vector.tensor_scalar(
+                out=work[i][:], in0=pre[i][:], scalar1=neg_mean[i][:], scalar2=inv_std[i][:],
+                op0=ALU.add, op1=ALU.mult,
+            )
+
+        def flip_hidden(i, flipped):
+            place = slice(P * (i % TILES_PER_BATCH), P * (i % TILES_PER_BATCH + 1))
+            for j in range(BLOCKS):
+                nc.tensor.transpose(flipped[j][:, place], work[i][:, P * j : P * (j + 1)], ident_f32[:])
+
+        def scale_on_scalar(out, in_, j):
+            nc.scalar.activation(
+                out=out, in_=in_, func=FUNC.Identity, bias=shift[:, j : j + 1], scale=gain[:, j : j + 1]
+            )
+
+        def scale_on_vector(out, in_, j):
+            nc.vector.tensor_scalar(
+                out=out, in0=in_, scalar1=gain[:, j : j + 1], scalar2=shift[:, j : j + 1],
+                op0=ALU.mult, op1=ALU.add,
+            )
+
+        def quantise_hidden(flipped, even_blocks):
+            planes = [
+                stage.tile([P, PACK, BANK], BF16, tag="planes%d" % c, name="planes%d" % c)
+                for c in range(PASSES)
+            ]
+            for j in range(BLOCKS):
+                scale = even_blocks if j % 2 == 0 else scale_on_vector
+                scale(planes[j // PACK][:, j % PACK, :], flipped[j][:], j)
+            grouped = [
+                stage.tile([P, BANK, PACK], BF16, align_bytes=64, tag="h1_grouped%d" % c, name="h1_grouped%d" % c)
+                for c in range(PASSES)
+            ]
+            codes = stage.tile([P, PASSES, BANK], U32, align_bytes=64, tag="h1_codes")
+            scales = stage.tile([P, PASSES, BANK], U8, align_bytes=64, tag="h1_scales")
+            for c in range(PASSES):
+                nc.vector.tensor_copy(
+                    out=grouped[c][:].rearrange("p (c i) t -> p c t i", i=4),
+                    in_=planes[c][:].rearrange("p t (c i) -> p c t i", i=4),
+                )
+            for c in range(PASSES):
+                nc.vector.quantize_mx(
+                    out=codes[:, c, :].bitcast(FP8X4), scales=scales[:, c, :],
+                    in_=grouped[c][:].rearrange("p b t -> p (b t)"),
+                )
+            return codes, scales
+
+        w2_codes = keep.tile([P, PASSES * ACTIONS], U32, align_bytes=64)
+        w2_scales = keep.tile([P, PASSES * ACTIONS], U8, align_bytes=64)
+        start_state = keep.tile([P, TILES, ACTIONS], F32)
+
+        def prepare_head():
+            w2_grouped = keep.tile([P, PASSES, ACTIONS, PACK], BF16, align_bytes=64)
+            nc.vector.tensor_copy(
+                out=w2_grouped[:], in_=w2_raw[:].rearrange("p (c t) a -> p c a t", t=PACK)
+            )
+            slope = keep.tile([P, TILES, ACTIONS], F32)
+            nc.vector.tensor_tensor(
+                out=slope[:], in0=k1_rows[:],
+                in1=bias2[:].unsqueeze(1).to_broadcast([P, TILES, ACTIONS]), op=ALU.add,
+            )
+            nc.vector.quantize_mx(
+                out=w2_codes[:].bitcast(FP8X4), scales=w2_scales[:],
+                in_=w2_grouped[:].rearrange("p c a t -> p (c a t)"),
+            )
+            nc.vector.scalar_tensor_tensor(
+                out=start_state[:], in0=slope[:], scalar=QUARTER, in1=z_rows[:],
+                op0=ALU.mult, op1=ALU.add,
+            )
+
+        def finish(n, codes, scales):
+            acc = psum.tile([P, TILES_PER_BATCH, ACTIONS], F32, tag="bank")
+            for r in range(TILES_PER_BATCH):
+                rows = slice(P * r, P * (r + 1))
+                for c in range(PASSES):
+                    cols = slice(ACTIONS * c, ACTIONS * (c + 1))
+                    nc.tensor.matmul_mx(
+                        out=acc[:, r, :],
+                        lhsT=codes[:, c, rows].bitcast(FP8X4),
+                        lhsT_scale=scales[:, c, rows],
+                        rhs=w2_codes[:, cols].bitcast(FP8X4),
+                        rhs_scale=w2_scales[:, cols],
+                        start=(c == 0),
+                        stop=(c == PASSES - 1),
+                    )
+            tiles = slice(TILES_PER_BATCH * n, TILES_PER_BATCH * (n + 1))
+            result = stage.tile([P, TILES_PER_BATCH, ACTIONS], F32, tag="result")
+            nc.vector.scalar_tensor_tensor(
+                out=result[:], in0=acc[:], scalar=QUARTER, in1=start_state[:, tiles, :],
+                op0=ALU.mult, op1=ALU.add,
+            )
+            nc.sync.dma_start(
+                out=out[BANK * n : BANK * (n + 1), :].rearrange("(r p) a -> p r a", p=P), in_=result[:]
+            )
+
+        batches = [
+            list(range(first, first + TILES_PER_BATCH)) for first in range(0, TILES, TILES_PER_BATCH)
+        ]
+        prepare(batches[0], nc.scalar.copy)
+        for i in batches[0]:
+            sigmoid(i)
+        for n, batch in enumerate(batches):
+            following = batches[n + 1] if n + 1 < len(batches) else []
+            prepare(following, nc.vector.tensor_copy)
+            if n == 0:
+                for i in batch:
+                    log(i)
+            if following:
+                nc.scalar.activation(out=warm[:], in_=smallest[:], func=FUNC.Sigmoid)
+            for i in batch:
+                tanh(i)
+                mish(i)
+            if n == 0:
+                prepare_head()
+            flipped = [psum.tile([P, BANK], F32, tag="bank", name="flipped%d" % j) for j in range(BLOCKS)]
+            for i in batch:
+                variance(i)
+                normalise(i)
+                flip_hidden(i, flipped)
+            for i in following:
+                sigmoid(i)
+            for i in following:
+                log(i)
+            codes, scales = quantise_hidden(flipped, scale_on_vector if following else scale_on_scalar)
+            finish(n, codes, scales)

@@ -24,7 +24,6 @@ LN_EPS = 1e-5
 ROOT_UNITS = 32.0
 QUARTER = 0.25
 SMALLEST = 2.0 ** -60
-TILES_PER_BATCH = BANK // P
 
 FLOPS = 2 * BATCH * UNITS * UNITS + 2 * BATCH * UNITS * ACTIONS
 
@@ -34,7 +33,8 @@ def tile_actorflowode_pb_kernel(tc, h0, z, k1, W1, b1, ln1_g, ln1_b, W2, b2, out
     with ExitStack() as ctx:
         keep = ctx.enter_context(tc.tile_pool(name="keep", bufs=1))
         stage = ctx.enter_context(tc.tile_pool(name="stage", bufs=2))
-        psum = ctx.enter_context(tc.psum_pool(name="psum", bufs=8))
+        psum = ctx.enter_context(tc.psum_pool(name="psum", bufs=6))
+        psum_head = ctx.enter_context(tc.psum_pool(name="psum_head", bufs=2))
         ctx.enter_context(tc.manual_schedule())
 
         smallest = keep.tile([P, 1], F32)
@@ -108,6 +108,17 @@ def tile_actorflowode_pb_kernel(tc, h0, z, k1, W1, b1, ln1_g, ln1_b, W2, b2, out
         nc.scalar.mul(out=gain[:], in_=norm_cols[:, 0:BLOCKS], mul=ROOT_UNITS)
         shift = keep.tile([P, BLOCKS], F32)
         nc.scalar.copy(out=shift[:], in_=norm_cols[:, BLOCKS : 2 * BLOCKS])
+
+        start_state = keep.tile([P, TILES, ACTIONS], F32)
+        slope = keep.tile([P, TILES, ACTIONS], F32)
+        nc.gpsimd.tensor_tensor(
+            out=slope[:], in0=k1_rows[:], in1=bias2[:].unsqueeze(1).to_broadcast([P, TILES, ACTIONS]),
+            op=ALU.add,
+        )
+        nc.gpsimd.tensor_scalar(
+            out=slope[:], in0=slope[:], scalar1=QUARTER, scalar2=0.0, op0=ALU.mult, op1=ALU.add
+        )
+        nc.gpsimd.tensor_tensor(out=start_state[:], in0=slope[:], in1=z_rows[:], op=ALU.add)
 
         w1_codes = keep.tile([P, PASSES, UNITS], U32, align_bytes=64)
         w1_scales = keep.tile([P, PASSES, UNITS], U8, align_bytes=64)
@@ -212,91 +223,91 @@ def tile_actorflowode_pb_kernel(tc, h0, z, k1, W1, b1, ln1_g, ln1_b, W2, b2, out
                 op0=ALU.mult, op1=ALU.add,
             )
 
-        def variance(i):
-            nc.scalar.activation(
-                out=work[i][:], in_=pre[i][:], func=FUNC.Square, bias=neg_mean[i][:],
-                accum_out=squares[i][:],
-            )
+        def variance(i, on_scalar):
+            if on_scalar:
+                nc.scalar.activation(
+                    out=work[i][:], in_=pre[i][:], func=FUNC.Square, bias=neg_mean[i][:],
+                    accum_out=squares[i][:],
+                )
+            else:
+                nc.vector.scalar_tensor_tensor(
+                    out=work[i][:], in0=pre[i][:], scalar=neg_mean[i][:], in1=pre[i][:],
+                    op0=ALU.add, op1=ALU.mult, accum_out=squares[i][:],
+                )
             nc.gpsimd.tensor_scalar(
                 out=padded[i][:], in0=squares[i][:], scalar1=1.0, scalar2=UNITS * LN_EPS,
                 op0=ALU.mult, op1=ALU.add,
             )
             nc.gpsimd.tensor_tensor(out=inv_std[i][:], in0=padded[i][:], in1=neg_half[:], op=ALU.pow)
 
-        def normalise(i):
-            nc.vector.tensor_scalar(
+        def normalise(i, engine):
+            engine.tensor_scalar(
                 out=work[i][:], in0=pre[i][:], scalar1=neg_mean[i][:], scalar2=inv_std[i][:],
                 op0=ALU.add, op1=ALU.mult,
             )
 
-        def flip_hidden(i, flipped):
-            place = slice(P * (i % TILES_PER_BATCH), P * (i % TILES_PER_BATCH + 1))
+        flipped = {}
+
+        def flip_hidden(i):
+            pair, place = i // 2, slice(P * (i % 2), P * (i % 2 + 1))
+            if i % 2 == 0:
+                flipped[pair] = [
+                    psum.tile([P, 2, 2 * P], F32, tag="bank", name="flipped%d" % k) for k in range(BLOCKS // 2)
+                ]
             for j in range(BLOCKS):
-                nc.tensor.transpose(flipped[j][:, place], work[i][:, P * j : P * (j + 1)], ident_f32[:])
+                nc.tensor.transpose(
+                    flipped[pair][j // 2][:, j % 2, place], work[i][:, P * j : P * (j + 1)], ident_f32[:]
+                )
 
-        def scale_on_scalar(out, in_, j):
-            nc.scalar.activation(
-                out=out, in_=in_, func=FUNC.Identity, bias=shift[:, j : j + 1], scale=gain[:, j : j + 1]
-            )
+        planes = {}
 
-        def scale_on_vector(out, in_, j):
-            nc.vector.tensor_scalar(
-                out=out, in0=in_, scalar1=gain[:, j : j + 1], scalar2=shift[:, j : j + 1],
-                op0=ALU.mult, op1=ALU.add,
-            )
-
-        def quantise_hidden(flipped, even_blocks):
-            planes = [
-                stage.tile([P, PACK, BANK], BF16, tag="planes%d" % c, name="planes%d" % c)
-                for c in range(PASSES)
-            ]
+        def scale_pair(pair, share):
+            planes[pair] = stage.tile([P, BLOCKS, 2 * P], BF16, tag="planes", name="planes")
             for j in range(BLOCKS):
-                scale = even_blocks if j % 2 == 0 else scale_on_vector
-                scale(planes[j // PACK][:, j % PACK, :], flipped[j][:], j)
-            grouped = [
-                stage.tile([P, BANK, PACK], BF16, align_bytes=64, tag="h1_grouped%d" % c, name="h1_grouped%d" % c)
-                for c in range(PASSES)
-            ]
-            codes = stage.tile([P, PASSES, BANK], U32, align_bytes=64, tag="h1_codes")
-            scales = stage.tile([P, PASSES, BANK], U8, align_bytes=64, tag="h1_scales")
-            for c in range(PASSES):
-                nc.vector.tensor_copy(
-                    out=grouped[c][:].rearrange("p (c i) t -> p c t i", i=4),
-                    in_=planes[c][:].rearrange("p t (c i) -> p c t i", i=4),
-                )
-            for c in range(PASSES):
-                nc.vector.quantize_mx(
-                    out=codes[:, c, :].bitcast(FP8X4), scales=scales[:, c, :],
-                    in_=grouped[c][:].rearrange("p b t -> p (b t)"),
-                )
-            return codes, scales
+                source = flipped[pair][j // 2][:, j % 2, :]
+                if share and (j // 2) % 2 == 0:
+                    nc.scalar.activation(
+                        out=planes[pair][:, j, :], in_=source, func=FUNC.Identity,
+                        bias=shift[:, j : j + 1], scale=gain[:, j : j + 1],
+                    )
+                else:
+                    nc.vector.tensor_scalar(
+                        out=planes[pair][:, j, :], in0=source,
+                        scalar1=gain[:, j : j + 1], scalar2=shift[:, j : j + 1],
+                        op0=ALU.mult, op1=ALU.add,
+                    )
 
         w2_codes = keep.tile([P, PASSES * ACTIONS], U32, align_bytes=64)
         w2_scales = keep.tile([P, PASSES * ACTIONS], U8, align_bytes=64)
-        start_state = keep.tile([P, TILES, ACTIONS], F32)
 
-        def prepare_head():
+        def quantise_w2():
             w2_grouped = keep.tile([P, PASSES, ACTIONS, PACK], BF16, align_bytes=64)
             nc.vector.tensor_copy(
                 out=w2_grouped[:], in_=w2_raw[:].rearrange("p (c t) a -> p c a t", t=PACK)
-            )
-            slope = keep.tile([P, TILES, ACTIONS], F32)
-            nc.vector.tensor_tensor(
-                out=slope[:], in0=k1_rows[:],
-                in1=bias2[:].unsqueeze(1).to_broadcast([P, TILES, ACTIONS]), op=ALU.add,
             )
             nc.vector.quantize_mx(
                 out=w2_codes[:].bitcast(FP8X4), scales=w2_scales[:],
                 in_=w2_grouped[:].rearrange("p c a t -> p (c a t)"),
             )
-            nc.vector.scalar_tensor_tensor(
-                out=start_state[:], in0=slope[:], scalar=QUARTER, in1=z_rows[:],
-                op0=ALU.mult, op1=ALU.add,
-            )
 
-        def finish(n, codes, scales):
-            acc = psum.tile([P, TILES_PER_BATCH, ACTIONS], F32, tag="bank")
-            for r in range(TILES_PER_BATCH):
+        head_sums = {}
+
+        def second_product(pair):
+            grouped = stage.tile([P, PASSES, 2 * P, PACK], BF16, align_bytes=64, tag="h1_grouped")
+            for c in range(PASSES):
+                nc.vector.tensor_copy(
+                    out=grouped[:, c, :, :].rearrange("p (c i) t -> p c t i", i=4),
+                    in_=planes[pair][:, PACK * c : PACK * (c + 1), :].rearrange("p t (c i) -> p c t i", i=4),
+                )
+            codes = stage.tile([P, PASSES, 2 * P], U32, align_bytes=64, tag="h1_codes")
+            scales = stage.tile([P, PASSES, 2 * P], U8, align_bytes=64, tag="h1_scales")
+            nc.vector.quantize_mx(
+                out=codes[:].rearrange("p c b -> p (c b)").bitcast(FP8X4),
+                scales=scales[:].rearrange("p c b -> p (c b)"),
+                in_=grouped[:].rearrange("p c b t -> p (c b t)"),
+            )
+            acc = psum_head.tile([P, 2, ACTIONS], F32, tag="head")
+            for r in range(2):
                 rows = slice(P * r, P * (r + 1))
                 for c in range(PASSES):
                     cols = slice(ACTIONS * c, ACTIONS * (c + 1))
@@ -309,43 +320,55 @@ def tile_actorflowode_pb_kernel(tc, h0, z, k1, W1, b1, ln1_g, ln1_b, W2, b2, out
                         start=(c == 0),
                         stop=(c == PASSES - 1),
                     )
-            tiles = slice(TILES_PER_BATCH * n, TILES_PER_BATCH * (n + 1))
-            result = stage.tile([P, TILES_PER_BATCH, ACTIONS], F32, tag="result")
+            head_sums[pair] = acc
+
+        def corrector(pair):
+            result = stage.tile([P, 2, ACTIONS], F32, tag="result")
             nc.vector.scalar_tensor_tensor(
-                out=result[:], in0=acc[:], scalar=QUARTER, in1=start_state[:, tiles, :],
-                op0=ALU.mult, op1=ALU.add,
+                out=result[:], in0=head_sums[pair][:], scalar=QUARTER,
+                in1=start_state[:, 2 * pair : 2 * pair + 2, :], op0=ALU.mult, op1=ALU.add,
             )
             nc.sync.dma_start(
-                out=out[BANK * n : BANK * (n + 1), :].rearrange("(r p) a -> p r a", p=P), in_=result[:]
+                out=out[2 * P * pair : 2 * P * (pair + 1), :].rearrange("(r p) a -> p r a", p=P),
+                in_=result[:],
             )
 
-        batches = [
-            list(range(first, first + TILES_PER_BATCH)) for first in range(0, TILES, TILES_PER_BATCH)
-        ]
-        prepare(batches[0], nc.scalar.copy)
-        for i in batches[0]:
+        first, last = range(0, TILES // 2), range(TILES // 2, TILES)
+        first_pairs, last_pairs = (0, 1), (2, 3)
+        prepare(first, nc.scalar.copy)
+        for i in first:
             sigmoid(i)
-        for n, batch in enumerate(batches):
-            following = batches[n + 1] if n + 1 < len(batches) else []
-            prepare(following, nc.vector.tensor_copy)
-            if n == 0:
-                for i in batch:
-                    log(i)
-            if following:
-                nc.scalar.activation(out=warm[:], in_=smallest[:], func=FUNC.Sigmoid)
-            for i in batch:
-                tanh(i)
-                mish(i)
-            if n == 0:
-                prepare_head()
-            flipped = [psum.tile([P, BANK], F32, tag="bank", name="flipped%d" % j) for j in range(BLOCKS)]
-            for i in batch:
-                variance(i)
-                normalise(i)
-                flip_hidden(i, flipped)
-            for i in following:
-                sigmoid(i)
-            for i in following:
-                log(i)
-            codes, scales = quantise_hidden(flipped, scale_on_vector if following else scale_on_scalar)
-            finish(n, codes, scales)
+        prepare(last, nc.vector.tensor_copy)
+        quantise_w2()
+        for i in first:
+            log(i)
+        nc.scalar.activation(out=warm[:], in_=smallest[:], func=FUNC.Sigmoid)
+        for i in first:
+            tanh(i)
+            mish(i)
+        for i in last:
+            sigmoid(i)
+        for i in last:
+            log(i)
+        for i in first:
+            variance(i, on_scalar=False)
+            normalise(i, nc.gpsimd)
+            flip_hidden(i)
+        for pair in first_pairs:
+            scale_pair(pair, share=False)
+        for i in last:
+            tanh(i)
+            mish(i)
+        for i in last:
+            variance(i, on_scalar=True)
+        for pair in last_pairs:
+            second_product(pair - 2)
+            for i in (2 * pair, 2 * pair + 1):
+                normalise(i, nc.vector)
+                flip_hidden(i)
+        for pair in last_pairs:
+            corrector(pair - 2)
+            scale_pair(pair, share=True)
+        for pair in last_pairs:
+            second_product(pair)
+            corrector(pair)

@@ -16,12 +16,12 @@ PACK = 4
 K_PASS = P * PACK
 BATCH, UNITS, ACTIONS = 1024, 1024, 128
 TILES = BATCH // P
+BATCH_TILES = TILES // 2
 PASSES = UNITS // K_PASS
 BANK = 512
 HALVES = UNITS // BANK
 BLOCKS = UNITS // P
 LN_EPS = 1e-5
-ROOT_UNITS = 32.0
 QUARTER = 0.25
 SMALLEST = 2.0 ** -60
 
@@ -33,14 +33,16 @@ def tile_actorflowode_pb_kernel(tc, h0, z, k1, W1, b1, ln1_g, ln1_b, W2, b2, out
     with ExitStack() as ctx:
         keep = ctx.enter_context(tc.tile_pool(name="keep", bufs=1))
         stage = ctx.enter_context(tc.tile_pool(name="stage", bufs=2))
-        psum = ctx.enter_context(tc.psum_pool(name="psum", bufs=6))
-        psum_head = ctx.enter_context(tc.psum_pool(name="psum_head", bufs=2))
+        psum = ctx.enter_context(tc.psum_pool(name="psum", bufs=7))
+        psum_head = ctx.enter_context(tc.psum_pool(name="psum_head", bufs=1))
         ctx.enter_context(tc.manual_schedule())
 
         smallest = keep.tile([P, 1], F32)
         nc.vector.memset(smallest[:], SMALLEST)
-        neg_half = keep.tile([P, 1], F32)
+        neg_half = keep.tile([P, 2], F32)
         nc.vector.memset(neg_half[:], -0.5)
+        eps = keep.tile([P, 1], F32)
+        nc.vector.memset(eps[:], LN_EPS)
         ones = keep.tile([P, P], BF16)
         nc.vector.memset(ones[:], 1.0)
         bias_rows = keep.tile([P, UNITS + 2 * ACTIONS], BF16)
@@ -105,7 +107,7 @@ def tile_actorflowode_pb_kernel(tc, h0, z, k1, W1, b1, ln1_g, ln1_b, W2, b2, out
         norm_cols = psum.tile([P, P], BF16, tag="bank")
         nc.tensor.transpose(norm_cols[:], norm_rows[:], ident_bf16[:])
         gain = keep.tile([P, BLOCKS], F32)
-        nc.scalar.mul(out=gain[:], in_=norm_cols[:, 0:BLOCKS], mul=ROOT_UNITS)
+        nc.scalar.copy(out=gain[:], in_=norm_cols[:, 0:BLOCKS])
         shift = keep.tile([P, BLOCKS], F32)
         nc.scalar.copy(out=shift[:], in_=norm_cols[:, BLOCKS : 2 * BLOCKS])
 
@@ -155,8 +157,10 @@ def tile_actorflowode_pb_kernel(tc, h0, z, k1, W1, b1, ln1_g, ln1_b, W2, b2, out
         h0_grouped = [
             keep.tile([P, UNITS], BF16, align_bytes=64, name="h0_grouped%d" % i) for i in range(TILES)
         ]
-        pre = [keep.tile([P, UNITS], F32, name="pre%d" % i) for i in range(TILES)]
-        work = [keep.tile([P, UNITS], F32, name="work%d" % i) for i in range(TILES)]
+        pre_batch = [keep.tile([P, BATCH_TILES, UNITS], F32, name="pre_batch%d" % n) for n in range(2)]
+        work_batch = [keep.tile([P, BATCH_TILES, UNITS], F32, name="work_batch%d" % n) for n in range(2)]
+        pre = [pre_batch[i // BATCH_TILES][:, i % BATCH_TILES, :] for i in range(TILES)]
+        work = [work_batch[i // BATCH_TILES][:, i % BATCH_TILES, :] for i in range(TILES)]
 
         def transpose_h0(i, copy):
             words = h0_raw[i][:].bitcast(F32)
@@ -198,52 +202,74 @@ def tile_actorflowode_pb_kernel(tc, h0, z, k1, W1, b1, ln1_g, ln1_b, W2, b2, out
             for i in batch:
                 first_product(i)
 
-        def sigmoid(i):
-            nc.scalar.activation(out=work[i][:], in_=pre[i][:], func=FUNC.Sigmoid, scale=-1.0)
+        def sigmoid(values, result):
+            nc.scalar.activation(out=result, in_=values, func=FUNC.Sigmoid, scale=-1.0)
 
-        def log(i):
-            nc.scalar.activation(out=work[i][:], in_=work[i][:], func=FUNC.Ln, bias=smallest[:])
+        def log(n):
+            nc.scalar.activation(out=work_batch[n][:], in_=work_batch[n][:], func=FUNC.Ln, bias=smallest[:])
 
         def tanh(i):
-            nc.scalar.activation(out=work[i][:], in_=work[i][:], func=FUNC.Tanh, scale=-1.0)
+            nc.scalar.activation(out=work[i], in_=work[i], func=FUNC.Tanh, scale=-1.0)
 
-        total = [keep.tile([P, 1], F32, name="total%d" % i) for i in range(TILES)]
-        neg_mean = [keep.tile([P, 1], F32, name="neg_mean%d" % i) for i in range(TILES)]
-        squares = [keep.tile([P, 1], F32, name="squares%d" % i) for i in range(TILES)]
-        padded = [keep.tile([P, 1], F32, name="padded%d" % i) for i in range(TILES)]
-        inv_std = [keep.tile([P, 1], F32, name="inv_std%d" % i) for i in range(TILES)]
-
-        def mish(i):
+        def mish(i, row_sum=None):
             nc.vector.scalar_tensor_tensor(
-                out=pre[i][:], in0=pre[i][:], scalar=1.0, in1=work[i][:],
-                op0=ALU.mult, op1=ALU.mult, accum_out=total[i][:],
-            )
-            nc.gpsimd.tensor_scalar(
-                out=neg_mean[i][:], in0=total[i][:], scalar1=-1.0 / UNITS, scalar2=0.0,
-                op0=ALU.mult, op1=ALU.add,
+                out=pre[i], in0=pre[i], scalar=1.0, in1=work[i],
+                op0=ALU.mult, op1=ALU.mult, accum_out=row_sum,
             )
 
-        def variance(i, on_scalar):
-            if on_scalar:
+        mean = {}
+        inv_std = {}
+        moments = {}
+
+        def tiles_of(pair):
+            return (2 * pair, 2 * pair + 1)
+
+        def inverse_std(pair, padded):
+            both = keep.tile([P, 2], F32, name="inv_std%d" % pair)
+            nc.gpsimd.tensor_tensor(out=both[:], in0=padded[:], in1=neg_half[:], op=ALU.pow)
+            for k, i in enumerate(tiles_of(pair)):
+                inv_std[i] = both[:, k : k + 1]
+
+        parts = {}
+
+        def partial_moments(i):
+            parts[i] = keep.tile([P, HALVES, 6], F32, name="parts%d" % i)
+            for half in range(HALVES):
+                nc.vector.bn_stats(out=parts[i][:, half, :], in_=pre[i][:, BANK * half : BANK * (half + 1)])
+
+        def join_moments(i):
+            pair, k = i // 2, i % 2
+            if k == 0:
+                moments[pair] = keep.tile([P, 2, 2], F32, name="moments%d" % pair)
+            nc.vector.bn_aggr(out=moments[pair][:, k, :], in_=parts[i][:].rearrange("p h s -> p (h s)"))
+            mean[i] = moments[pair][:, k, 0:1]
+
+        def inverse_std_after_vector(pair):
+            padded = keep.tile([P, 2], F32, name="padded%d" % pair)
+            nc.vector.tensor_scalar_add(out=padded[:], in0=moments[pair][:, :, 1], scalar1=LN_EPS)
+            inverse_std(pair, padded)
+
+        def statistics_on_scalar(pair, row_sums):
+            squares = keep.tile([P, 2], F32, name="squares%d" % pair)
+            for k, i in enumerate(tiles_of(pair)):
                 nc.scalar.activation(
-                    out=work[i][:], in_=pre[i][:], func=FUNC.Square, bias=neg_mean[i][:],
-                    accum_out=squares[i][:],
+                    out=work[i], in_=pre[i], func=FUNC.Square, bias=row_sums[:, k : k + 1],
+                    scale=-1.0 * UNITS, accum_out=squares[:, k : k + 1],
                 )
-            else:
-                nc.vector.scalar_tensor_tensor(
-                    out=work[i][:], in0=pre[i][:], scalar=neg_mean[i][:], in1=pre[i][:],
-                    op0=ALU.add, op1=ALU.mult, accum_out=squares[i][:],
-                )
-            nc.gpsimd.tensor_scalar(
-                out=padded[i][:], in0=squares[i][:], scalar1=1.0, scalar2=UNITS * LN_EPS,
-                op0=ALU.mult, op1=ALU.add,
+            means = keep.tile([P, 2], F32, name="means%d" % pair)
+            nc.scalar.mul(out=means[:], in_=row_sums[:], mul=1.0 / UNITS)
+            for k, i in enumerate(tiles_of(pair)):
+                mean[i] = means[:, k : k + 1]
+            padded = keep.tile([P, 2], F32, name="padded%d" % pair)
+            nc.scalar.activation(
+                out=padded[:], in_=squares[:], func=FUNC.Identity, bias=eps[:], scale=1.0 / UNITS ** 3
             )
-            nc.gpsimd.tensor_tensor(out=inv_std[i][:], in0=padded[i][:], in1=neg_half[:], op=ALU.pow)
+            inverse_std(pair, padded)
 
-        def normalise(i, engine):
-            engine.tensor_scalar(
-                out=work[i][:], in0=pre[i][:], scalar1=neg_mean[i][:], scalar2=inv_std[i][:],
-                op0=ALU.add, op1=ALU.mult,
+        def normalise(i):
+            nc.vector.tensor_scalar(
+                out=work[i], in0=pre[i], scalar1=mean[i], scalar2=inv_std[i],
+                op0=ALU.subtract, op1=ALU.mult,
             )
 
         flipped = {}
@@ -261,11 +287,12 @@ def tile_actorflowode_pb_kernel(tc, h0, z, k1, W1, b1, ln1_g, ln1_b, W2, b2, out
 
         planes = {}
 
-        def scale_pair(pair, share):
-            planes[pair] = stage.tile([P, BLOCKS, 2 * P], BF16, tag="planes", name="planes")
-            for j in range(BLOCKS):
+        def scale_pair(pair, c, on_scalar):
+            if c == 0:
+                planes[pair] = stage.tile([P, BLOCKS, 2 * P], BF16, tag="planes", name="planes")
+            for j in range(PACK * c, PACK * (c + 1)):
                 source = flipped[pair][j // 2][:, j % 2, :]
-                if share and (j // 2) % 2 == 0:
+                if on_scalar:
                     nc.scalar.activation(
                         out=planes[pair][:, j, :], in_=source, func=FUNC.Identity,
                         bias=shift[:, j : j + 1], scale=gain[:, j : j + 1],
@@ -292,13 +319,19 @@ def tile_actorflowode_pb_kernel(tc, h0, z, k1, W1, b1, ln1_g, ln1_b, W2, b2, out
 
         head_sums = {}
 
-        def second_product(pair):
+        h1_grouped = {}
+
+        def regroup(pair):
             grouped = stage.tile([P, PASSES, 2 * P, PACK], BF16, align_bytes=64, tag="h1_grouped")
             for c in range(PASSES):
                 nc.vector.tensor_copy(
                     out=grouped[:, c, :, :].rearrange("p (c i) t -> p c t i", i=4),
                     in_=planes[pair][:, PACK * c : PACK * (c + 1), :].rearrange("p t (c i) -> p c t i", i=4),
                 )
+            h1_grouped[pair] = grouped
+
+        def second_product(pair):
+            grouped = h1_grouped[pair]
             codes = stage.tile([P, PASSES, 2 * P], U32, align_bytes=64, tag="h1_codes")
             scales = stage.tile([P, PASSES, 2 * P], U8, align_bytes=64, tag="h1_scales")
             nc.vector.quantize_mx(
@@ -306,13 +339,14 @@ def tile_actorflowode_pb_kernel(tc, h0, z, k1, W1, b1, ln1_g, ln1_b, W2, b2, out
                 scales=scales[:].rearrange("p c b -> p (c b)"),
                 in_=grouped[:].rearrange("p c b t -> p (c b t)"),
             )
-            acc = psum_head.tile([P, 2, ACTIONS], F32, tag="head")
+            if pair % 2 == 0:
+                head_sums[pair // 2] = psum_head.tile([P, 4, ACTIONS], F32, tag="head", name="head_sums")
             for r in range(2):
                 rows = slice(P * r, P * (r + 1))
                 for c in range(PASSES):
                     cols = slice(ACTIONS * c, ACTIONS * (c + 1))
                     nc.tensor.matmul_mx(
-                        out=acc[:, r, :],
+                        out=head_sums[pair // 2][:, 2 * (pair % 2) + r, :],
                         lhsT=codes[:, c, rows].bitcast(FP8X4),
                         lhsT_scale=scales[:, c, rows],
                         rhs=w2_codes[:, cols].bitcast(FP8X4),
@@ -320,12 +354,11 @@ def tile_actorflowode_pb_kernel(tc, h0, z, k1, W1, b1, ln1_g, ln1_b, W2, b2, out
                         start=(c == 0),
                         stop=(c == PASSES - 1),
                     )
-            head_sums[pair] = acc
 
         def corrector(pair):
             result = stage.tile([P, 2, ACTIONS], F32, tag="result")
             nc.vector.scalar_tensor_tensor(
-                out=result[:], in0=head_sums[pair][:], scalar=QUARTER,
+                out=result[:], in0=head_sums[pair // 2][:, 2 * (pair % 2) : 2 * (pair % 2) + 2, :], scalar=QUARTER,
                 in1=start_state[:, 2 * pair : 2 * pair + 2, :], op0=ALU.mult, op1=ALU.add,
             )
             nc.sync.dma_start(
@@ -337,38 +370,53 @@ def tile_actorflowode_pb_kernel(tc, h0, z, k1, W1, b1, ln1_g, ln1_b, W2, b2, out
         first_pairs, last_pairs = (0, 1), (2, 3)
         prepare(first, nc.scalar.copy)
         for i in first:
-            sigmoid(i)
+            sigmoid(pre[i], work[i])
         prepare(last, nc.vector.tensor_copy)
         quantise_w2()
-        for i in first:
-            log(i)
+        log(0)
         nc.scalar.activation(out=warm[:], in_=smallest[:], func=FUNC.Sigmoid)
         for i in first:
             tanh(i)
             mish(i)
-        for i in last:
-            sigmoid(i)
-        for i in last:
-            log(i)
-        for i in first:
-            variance(i, on_scalar=False)
-            normalise(i, nc.gpsimd)
-            flip_hidden(i)
-        for pair in first_pairs:
-            scale_pair(pair, share=False)
+            if i >= 1:
+                partial_moments(i - 1)
+            if i >= 2:
+                join_moments(i - 2)
+        sigmoid(pre_batch[1][:], work_batch[1][:])
+        log(1)
+        partial_moments(3)
+        inverse_std_after_vector(0)
+        join_moments(2)
+        normalise(0)
+        flip_hidden(0)
+        join_moments(3)
+        normalise(1)
+        flip_hidden(1)
+        inverse_std_after_vector(1)
+        normalise(2)
+        flip_hidden(2)
+        normalise(3)
+        flip_hidden(3)
+        for c in range(PASSES):
+            scale_pair(0, c, on_scalar=False)
+        regroup(0)
+        row_sums = {pair: keep.tile([P, 2], F32, name="row_sums%d" % pair) for pair in last_pairs}
         for i in last:
             tanh(i)
-            mish(i)
-        for i in last:
-            variance(i, on_scalar=True)
-        for pair in last_pairs:
-            second_product(pair - 2)
-            for i in (2 * pair, 2 * pair + 1):
-                normalise(i, nc.vector)
+            mish(i, row_sum=row_sums[i // 2][:, i % 2 : i % 2 + 1])
+            if i == last[0]:
+                second_product(0)
+        for c, pair in enumerate(last_pairs):
+            statistics_on_scalar(pair, row_sums[pair])
+            scale_pair(1, c, on_scalar=False)
+            for i in tiles_of(pair):
+                normalise(i)
                 flip_hidden(i)
-        for pair in last_pairs:
-            corrector(pair - 2)
-            scale_pair(pair, share=True)
-        for pair in last_pairs:
+        for pair in (1, 2, 3):
+            if pair in last_pairs:
+                for c in range(PASSES):
+                    scale_pair(pair, c, on_scalar=True)
+            regroup(pair)
+            corrector(pair - 1)
             second_product(pair)
-            corrector(pair)
+        corrector(3)

@@ -366,8 +366,9 @@ def tile_actorflowode_pb_kernel(tc, h0, z, k1, W1, b1, ln1_g, ln1_b, W2, b2, out
                 in_=result[:],
             )
 
-        first, last = range(0, TILES // 2), range(TILES // 2, TILES)
-        first_pairs, last_pairs = (0, 1), (2, 3)
+        first, last = range(0, BATCH_TILES), range(BATCH_TILES, TILES)
+        pair_a, pair_b = 0, 1
+        pair_c, pair_d = 2, 3
         prepare(first, nc.scalar.copy)
         for i in first:
             sigmoid(pre[i], work[i])
@@ -378,45 +379,51 @@ def tile_actorflowode_pb_kernel(tc, h0, z, k1, W1, b1, ln1_g, ln1_b, W2, b2, out
         for i in first:
             tanh(i)
             mish(i)
-            if i >= 1:
-                partial_moments(i - 1)
-            if i >= 2:
+            if i - 2 in first:
                 join_moments(i - 2)
+            if i - 1 in first:
+                partial_moments(i - 1)
         sigmoid(pre_batch[1][:], work_batch[1][:])
         log(1)
+        inverse_std_after_vector(pair_a)
         partial_moments(3)
-        inverse_std_after_vector(0)
         join_moments(2)
         normalise(0)
         flip_hidden(0)
         join_moments(3)
         normalise(1)
         flip_hidden(1)
-        inverse_std_after_vector(1)
+        inverse_std_after_vector(pair_b)
         normalise(2)
         flip_hidden(2)
         normalise(3)
         flip_hidden(3)
         for c in range(PASSES):
-            scale_pair(0, c, on_scalar=False)
-        regroup(0)
-        row_sums = {pair: keep.tile([P, 2], F32, name="row_sums%d" % pair) for pair in last_pairs}
+            scale_pair(pair_a, c, on_scalar=False)
+        regroup(pair_a)
+        row_sums = {pair: keep.tile([P, 2], F32, name="row_sums%d" % pair) for pair in (pair_c, pair_d)}
         for i in last:
             tanh(i)
             mish(i, row_sum=row_sums[i // 2][:, i % 2 : i % 2 + 1])
             if i == last[0]:
-                second_product(0)
-        for c, pair in enumerate(last_pairs):
-            statistics_on_scalar(pair, row_sums[pair])
-            scale_pair(1, c, on_scalar=False)
-            for i in tiles_of(pair):
-                normalise(i)
-                flip_hidden(i)
-        for pair in (1, 2, 3):
-            if pair in last_pairs:
-                for c in range(PASSES):
-                    scale_pair(pair, c, on_scalar=True)
+                second_product(pair_a)
+        statistics_on_scalar(pair_c, row_sums[pair_c])
+        scale_pair(pair_b, 0, on_scalar=False)
+        statistics_on_scalar(pair_d, row_sums[pair_d])
+        scale_pair(pair_b, 1, on_scalar=True)
+        for i in tiles_of(pair_c):
+            normalise(i)
+            flip_hidden(i)
+        corrector(pair_a)
+        for i in tiles_of(pair_d):
+            normalise(i)
+            flip_hidden(i)
+        regroup(pair_b)
+        second_product(pair_b)
+        for pair in (pair_c, pair_d):
+            for c in range(PASSES):
+                scale_pair(pair, c, on_scalar=True)
             regroup(pair)
             corrector(pair - 1)
             second_product(pair)
-        corrector(3)
+        corrector(pair_d)

from contextlib import ExitStack

import concourse.mybir as mybir
from concourse.masks import make_identity

F32 = mybir.dt.float32
BF16 = mybir.dt.bfloat16
U32 = mybir.dt.uint32
U8 = mybir.dt.uint8
FP8X4 = mybir.dt.float8_e4m3fn_x4
FUNC = mybir.ActivationFunctionType
ALU = mybir.AluOpType

P = 128
PACK = 4
K_PASS = P * PACK
BATCH, UNITS, ACTIONS = 1024, 1024, 128
TILES = BATCH // P
BATCH_TILES = TILES // 2
PASSES = UNITS // K_PASS
BANK = 512
HALVES = UNITS // BANK
BLOCKS = UNITS // P
LN_EPS = 1e-5
QUARTER = 0.25
SMALLEST = 2.0 ** -60

FLOPS = 2 * BATCH * UNITS * UNITS + 2 * BATCH * UNITS * ACTIONS


def tile_actorflowode_pb_kernel(tc, h0, z, k1, W1, b1, ln1_g, ln1_b, W2, b2, out):
    nc = tc.nc
    with ExitStack() as ctx:
        keep = ctx.enter_context(tc.tile_pool(name="keep", bufs=1))
        stage = ctx.enter_context(tc.tile_pool(name="stage", bufs=2))
        psum = ctx.enter_context(tc.psum_pool(name="psum", bufs=7))
        psum_head = ctx.enter_context(tc.psum_pool(name="psum_head", bufs=1))
        ctx.enter_context(tc.manual_schedule())

        smallest = keep.tile([P, 1], F32)
        nc.vector.memset(smallest[:], SMALLEST)
        neg_half = keep.tile([P, 2], F32)
        nc.vector.memset(neg_half[:], -0.5)
        eps = keep.tile([P, 1], F32)
        nc.vector.memset(eps[:], LN_EPS)
        ones = keep.tile([P, P], BF16)
        nc.vector.memset(ones[:], 1.0)
        bias_rows = keep.tile([P, UNITS + 2 * ACTIONS], BF16)
        nc.vector.memset(bias_rows[:], 0.0)
        norm_rows = keep.tile([P, P], BF16)
        nc.vector.memset(norm_rows[:], 0.0)
        ident_f32 = keep.tile([P, P], F32)
        make_identity(nc, ident_f32[:])
        ident_bf16 = keep.tile([P, P], BF16)
        make_identity(nc, ident_bf16[:])

        nc.scalar.dma_start(out=bias_rows[0:1, 0:UNITS], in_=b1.rearrange("(o n) -> o n", o=1))
        nc.scalar.dma_start(
            out=bias_rows[0:1, UNITS : UNITS + ACTIONS], in_=b2.rearrange("(o n) -> o n", o=1)
        )
        nc.scalar.dma_start(out=norm_rows[0:BLOCKS, :], in_=ln1_g.rearrange("(j p) -> j p", p=P))
        nc.scalar.dma_start(
            out=norm_rows[BLOCKS : 2 * BLOCKS, :], in_=ln1_b.rearrange("(j p) -> j p", p=P)
        )

        warm = keep.tile([P, 1], F32)
        nc.scalar.activation(out=warm[:], in_=smallest[:], func=FUNC.Sigmoid)

        w1_raw = keep.tile([P, PASSES, PACK, UNITS], BF16)

        def load_w1(half, g):
            cols = slice(BANK * half, BANK * (half + 1))
            for u in range(2):
                first = K_PASS * g + 2 * P * u
                nc.sync.dma_start(
                    out=w1_raw[:, g, 2 * u : 2 * u + 2, cols],
                    in_=W1[first : first + 2 * P, cols].rearrange("(p e) n -> p e n", e=2),
                )

        h0_raw = [keep.tile([P, UNITS], BF16, name="h0_raw%d" % i) for i in range(TILES)]

        def load_h0(i):
            nc.sync.dma_start(out=h0_raw[i][:], in_=h0[P * i : P * (i + 1), :])

        for half in range(HALVES):
            for g in range(PASSES):
                load_w1(half, g)
        for i in range(TILES):
            load_h0(i)
        w2_raw = keep.tile([P, BLOCKS, ACTIONS], BF16)
        nc.sync.dma_start(out=w2_raw[:], in_=W2.rearrange("(j p) a -> p j a", p=P))
        z_rows = keep.tile([P, TILES, ACTIONS], BF16)
        nc.sync.dma_start(out=z_rows[:], in_=z.rearrange("(i p) a -> p i a", p=P))
        k1_rows = keep.tile([P, TILES, ACTIONS], BF16)
        nc.sync.dma_start(out=k1_rows[:], in_=k1.rearrange("(i p) a -> p i a", p=P))

        bias1 = keep.tile([P, UNITS], BF16)
        for half in range(HALVES):
            cols = slice(BANK * half, BANK * (half + 1))
            spread = psum.tile([P, BANK], F32, tag="bank")
            nc.tensor.matmul(out=spread[:], lhsT=ones[:], rhs=bias_rows[:, cols], start=True, stop=True)
            nc.scalar.copy(out=bias1[:, cols], in_=spread[:])
        bias2 = keep.tile([P, ACTIONS], F32)
        spread = psum.tile([P, 2 * ACTIONS], F32, tag="bank")
        nc.tensor.matmul(out=spread[:], lhsT=ones[:], rhs=bias_rows[:, UNITS:], start=True, stop=True)
        nc.scalar.copy(out=bias2[:], in_=spread[:, 0:ACTIONS])
        norm_cols = psum.tile([P, P], BF16, tag="bank")
        nc.tensor.transpose(norm_cols[:], norm_rows[:], ident_bf16[:])
        gain = keep.tile([P, BLOCKS], F32)
        nc.scalar.copy(out=gain[:], in_=norm_cols[:, 0:BLOCKS])
        shift = keep.tile([P, BLOCKS], F32)
        nc.scalar.copy(out=shift[:], in_=norm_cols[:, BLOCKS : 2 * BLOCKS])

        start_state = keep.tile([P, TILES, ACTIONS], F32)
        slope = keep.tile([P, TILES, ACTIONS], F32)
        nc.gpsimd.tensor_tensor(
            out=slope[:], in0=k1_rows[:], in1=bias2[:].unsqueeze(1).to_broadcast([P, TILES, ACTIONS]),
            op=ALU.add,
        )
        nc.gpsimd.tensor_scalar(
            out=slope[:], in0=slope[:], scalar1=QUARTER, scalar2=0.0, op0=ALU.mult, op1=ALU.add
        )
        nc.gpsimd.tensor_tensor(out=start_state[:], in0=slope[:], in1=z_rows[:], op=ALU.add)

        w1_codes = keep.tile([P, PASSES, UNITS], U32, align_bytes=64)
        w1_scales = keep.tile([P, PASSES, UNITS], U8, align_bytes=64)
        w1_grouped = {}

        def regroup_w1(half, g):
            cols = slice(BANK * half, BANK * (half + 1))
            grouped = keep.tile([P, BANK, PACK], BF16, align_bytes=64, name="w1_grouped%d%d" % (half, g))
            nc.vector.tensor_copy(
                out=grouped[:].rearrange("p (c i) t -> p c t i", i=4),
                in_=w1_raw[:, g, :, cols].rearrange("p t (c i) -> p c t i", i=4),
            )
            w1_grouped[(half, g)] = grouped

        def quantise_w1(half, g):
            cols = slice(BANK * half, BANK * (half + 1))
            nc.vector.quantize_mx(
                out=w1_codes[:, g, cols].bitcast(FP8X4),
                scales=w1_scales[:, g, cols],
                in_=w1_grouped[(half, g)][:].rearrange("p n t -> p (n t)"),
            )

        regroup_w1(0, 0)
        regroup_w1(0, 1)
        quantise_w1(0, 0)
        regroup_w1(1, 0)
        quantise_w1(0, 1)
        regroup_w1(1, 1)
        quantise_w1(1, 0)
        quantise_w1(1, 1)

        h0_codes = keep.tile([P, TILES, PASSES * P], U32, align_bytes=64)
        h0_scales = keep.tile([P, TILES, PASSES * P], U8, align_bytes=64)
        h0_grouped = [
            keep.tile([P, UNITS], BF16, align_bytes=64, name="h0_grouped%d" % i) for i in range(TILES)
        ]
        pre_batch = [keep.tile([P, BATCH_TILES, UNITS], F32, name="pre_batch%d" % n) for n in range(2)]
        work_batch = [keep.tile([P, BATCH_TILES, UNITS], F32, name="work_batch%d" % n) for n in range(2)]
        pre = [pre_batch[i // BATCH_TILES][:, i % BATCH_TILES, :] for i in range(TILES)]
        work = [work_batch[i // BATCH_TILES][:, i % BATCH_TILES, :] for i in range(TILES)]

        def transpose_h0(i, copy):
            words = h0_raw[i][:].bitcast(F32)
            flipped = psum.tile([P, PACK, P], F32, tag="bank")
            for j in range(PACK):
                nc.tensor.transpose(flipped[:, j, :], words[:, P * j : P * (j + 1)], ident_f32[:])
            copy(
                out=h0_grouped[i][:].bitcast(F32).rearrange("p (g b u) -> p g b u", g=PASSES, u=2),
                in_=flipped[:].rearrange("p (g u) b -> p g b u", u=2),
            )

        def quantise_h0(i):
            nc.vector.quantize_mx(
                out=h0_codes[:, i, :].bitcast(FP8X4), scales=h0_scales[:, i, :], in_=h0_grouped[i][:]
            )

        def first_product(i):
            for half in range(HALVES):
                cols = slice(BANK * half, BANK * (half + 1))
                acc = psum.tile([P, BANK], F32, tag="bank")
                for g in range(PASSES):
                    rows = slice(P * g, P * (g + 1))
                    nc.tensor.matmul_mx(
                        out=acc[:],
                        lhsT=h0_codes[:, i, rows].bitcast(FP8X4),
                        lhsT_scale=h0_scales[:, i, rows],
                        rhs=w1_codes[:, g, cols].bitcast(FP8X4),
                        rhs_scale=w1_scales[:, g, cols],
                        start=(g == 0),
                        stop=(g == PASSES - 1),
                    )
                nc.vector.tensor_tensor(out=pre[i][:, cols], in0=acc[:], in1=bias1[:, cols], op=ALU.add)

        def prepare(batch, copy):
            for i in batch:
                transpose_h0(i, copy)
            for i in batch:
                quantise_h0(i)
            for i in batch:
                first_product(i)

        def sigmoid(values, result):
            nc.scalar.activation(out=result, in_=values, func=FUNC.Sigmoid, scale=-1.0)

        def log(n):
            nc.scalar.activation(out=work_batch[n][:], in_=work_batch[n][:], func=FUNC.Ln, bias=smallest[:])

        def tanh(i):
            nc.scalar.activation(out=work[i], in_=work[i], func=FUNC.Tanh, scale=-1.0)

        def mish(i, row_sum=None):
            nc.vector.scalar_tensor_tensor(
                out=pre[i], in0=pre[i], scalar=1.0, in1=work[i],
                op0=ALU.mult, op1=ALU.mult, accum_out=row_sum,
            )

        mean = {}
        inv_std = {}
        moments = {}

        def tiles_of(pair):
            return (2 * pair, 2 * pair + 1)

        def inverse_std(pair, padded):
            both = keep.tile([P, 2], F32, name="inv_std%d" % pair)
            nc.gpsimd.tensor_tensor(out=both[:], in0=padded[:], in1=neg_half[:], op=ALU.pow)
            for k, i in enumerate(tiles_of(pair)):
                inv_std[i] = both[:, k : k + 1]

        parts = {}

        def partial_moments(i):
            parts[i] = keep.tile([P, HALVES, 6], F32, name="parts%d" % i)
            for half in range(HALVES):
                nc.vector.bn_stats(out=parts[i][:, half, :], in_=pre[i][:, BANK * half : BANK * (half + 1)])

        def join_moments(i):
            pair, k = i // 2, i % 2
            if k == 0:
                moments[pair] = keep.tile([P, 2, 2], F32, name="moments%d" % pair)
            nc.vector.bn_aggr(out=moments[pair][:, k, :], in_=parts[i][:].rearrange("p h s -> p (h s)"))
            mean[i] = moments[pair][:, k, 0:1]

        def inverse_std_after_vector(pair):
            padded = keep.tile([P, 2], F32, name="padded%d" % pair)
            nc.vector.tensor_scalar_add(out=padded[:], in0=moments[pair][:, :, 1], scalar1=LN_EPS)
            inverse_std(pair, padded)

        def statistics_on_scalar(pair, row_sums):
            squares = keep.tile([P, 2], F32, name="squares%d" % pair)
            for k, i in enumerate(tiles_of(pair)):
                nc.scalar.activation(
                    out=work[i], in_=pre[i], func=FUNC.Square, bias=row_sums[:, k : k + 1],
                    scale=-1.0 * UNITS, accum_out=squares[:, k : k + 1],
                )
            means = keep.tile([P, 2], F32, name="means%d" % pair)
            nc.scalar.mul(out=means[:], in_=row_sums[:], mul=1.0 / UNITS)
            for k, i in enumerate(tiles_of(pair)):
                mean[i] = means[:, k : k + 1]
            padded = keep.tile([P, 2], F32, name="padded%d" % pair)
            nc.scalar.activation(
                out=padded[:], in_=squares[:], func=FUNC.Identity, bias=eps[:], scale=1.0 / UNITS ** 3
            )
            inverse_std(pair, padded)

        def normalise(i):
            nc.vector.tensor_scalar(
                out=work[i], in0=pre[i], scalar1=mean[i], scalar2=inv_std[i],
                op0=ALU.subtract, op1=ALU.mult,
            )

        flipped = {}

        def flip_hidden(i):
            pair, place = i // 2, slice(P * (i % 2), P * (i % 2 + 1))
            if i % 2 == 0:
                flipped[pair] = [
                    psum.tile([P, 2, 2 * P], F32, tag="bank", name="flipped%d" % k) for k in range(BLOCKS // 2)
                ]
            for j in range(BLOCKS):
                nc.tensor.transpose(
                    flipped[pair][j // 2][:, j % 2, place], work[i][:, P * j : P * (j + 1)], ident_f32[:]
                )

        planes = {}

        def scale_pair(pair, c, on_scalar):
            if c == 0:
                planes[pair] = stage.tile([P, BLOCKS, 2 * P], BF16, tag="planes", name="planes")
            for j in range(PACK * c, PACK * (c + 1)):
                source = flipped[pair][j // 2][:, j % 2, :]
                if on_scalar:
                    nc.scalar.activation(
                        out=planes[pair][:, j, :], in_=source, func=FUNC.Identity,
                        bias=shift[:, j : j + 1], scale=gain[:, j : j + 1],
                    )
                else:
                    nc.vector.tensor_scalar(
                        out=planes[pair][:, j, :], in0=source,
                        scalar1=gain[:, j : j + 1], scalar2=shift[:, j : j + 1],
                        op0=ALU.mult, op1=ALU.add,
                    )

        w2_codes = keep.tile([P, PASSES * ACTIONS], U32, align_bytes=64)
        w2_scales = keep.tile([P, PASSES * ACTIONS], U8, align_bytes=64)

        def quantise_w2():
            w2_grouped = keep.tile([P, PASSES, ACTIONS, PACK], BF16, align_bytes=64)
            nc.vector.tensor_copy(
                out=w2_grouped[:], in_=w2_raw[:].rearrange("p (c t) a -> p c a t", t=PACK)
            )
            nc.vector.quantize_mx(
                out=w2_codes[:].bitcast(FP8X4), scales=w2_scales[:],
                in_=w2_grouped[:].rearrange("p c a t -> p (c a t)"),
            )

        head_sums = {}

        h1_grouped = {}

        def regroup(pair):
            grouped = stage.tile([P, PASSES, 2 * P, PACK], BF16, align_bytes=64, tag="h1_grouped")
            for c in range(PASSES):
                nc.vector.tensor_copy(
                    out=grouped[:, c, :, :].rearrange("p (c i) t -> p c t i", i=4),
                    in_=planes[pair][:, PACK * c : PACK * (c + 1), :].rearrange("p t (c i) -> p c t i", i=4),
                )
            h1_grouped[pair] = grouped

        def second_product(pair):
            grouped = h1_grouped[pair]
            codes = stage.tile([P, PASSES, 2 * P], U32, align_bytes=64, tag="h1_codes")
            scales = stage.tile([P, PASSES, 2 * P], U8, align_bytes=64, tag="h1_scales")
            nc.vector.quantize_mx(
                out=codes[:].rearrange("p c b -> p (c b)").bitcast(FP8X4),
                scales=scales[:].rearrange("p c b -> p (c b)"),
                in_=grouped[:].rearrange("p c b t -> p (c b t)"),
            )
            if pair % 2 == 0:
                head_sums[pair // 2] = psum_head.tile([P, 4, ACTIONS], F32, tag="head", name="head_sums")
            for r in range(2):
                rows = slice(P * r, P * (r + 1))
                for c in range(PASSES):
                    cols = slice(ACTIONS * c, ACTIONS * (c + 1))
                    nc.tensor.matmul_mx(
                        out=head_sums[pair // 2][:, 2 * (pair % 2) + r, :],
                        lhsT=codes[:, c, rows].bitcast(FP8X4),
                        lhsT_scale=scales[:, c, rows],
                        rhs=w2_codes[:, cols].bitcast(FP8X4),
                        rhs_scale=w2_scales[:, cols],
                        start=(c == 0),
                        stop=(c == PASSES - 1),
                    )

        def corrector(pair):
            result = stage.tile([P, 2, ACTIONS], F32, tag="result")
            nc.vector.scalar_tensor_tensor(
                out=result[:], in0=head_sums[pair // 2][:, 2 * (pair % 2) : 2 * (pair % 2) + 2, :], scalar=QUARTER,
                in1=start_state[:, 2 * pair : 2 * pair + 2, :], op0=ALU.mult, op1=ALU.add,
            )
            nc.sync.dma_start(
                out=out[2 * P * pair : 2 * P * (pair + 1), :].rearrange("(r p) a -> p r a", p=P),
                in_=result[:],
            )

        first, last = range(0, BATCH_TILES), range(BATCH_TILES, TILES)
        pair_a, pair_b = 0, 1
        pair_c, pair_d = 2, 3
        prepare(first, nc.scalar.copy)
        for i in first:
            sigmoid(pre[i], work[i])
        prepare(last, nc.vector.tensor_copy)
        quantise_w2()
        log(0)
        nc.scalar.activation(out=warm[:], in_=smallest[:], func=FUNC.Sigmoid)
        for i in first:
            tanh(i)
            mish(i)
            if i - 2 in first:
                join_moments(i - 2)
            if i - 1 in first:
                partial_moments(i - 1)
        sigmoid(pre_batch[1][:], work_batch[1][:])
        log(1)
        inverse_std_after_vector(pair_a)
        partial_moments(3)
        join_moments(2)
        normalise(0)
        flip_hidden(0)
        join_moments(3)
        normalise(1)
        flip_hidden(1)
        inverse_std_after_vector(pair_b)
        normalise(2)
        flip_hidden(2)
        normalise(3)
        flip_hidden(3)
        for c in range(PASSES):
            scale_pair(pair_a, c, on_scalar=False)
        regroup(pair_a)
        row_sums = {pair: keep.tile([P, 2], F32, name="row_sums%d" % pair) for pair in (pair_c, pair_d)}
        for i in last:
            tanh(i)
            mish(i, row_sum=row_sums[i // 2][:, i % 2 : i % 2 + 1])
            if i == last[0]:
                second_product(pair_a)
        statistics_on_scalar(pair_c, row_sums[pair_c])
        scale_pair(pair_b, 0, on_scalar=False)
        statistics_on_scalar(pair_d, row_sums[pair_d])
        scale_pair(pair_b, 1, on_scalar=True)
        for i in tiles_of(pair_c):
            normalise(i)
            flip_hidden(i)
        corrector(pair_a)
        for i in tiles_of(pair_d):
            normalise(i)
            flip_hidden(i)
        regroup(pair_b)
        second_product(pair_b)
        for pair in (pair_c, pair_d):
            for c in range(PASSES):
                scale_pair(pair, c, on_scalar=True)
            regroup(pair)
            corrector(pair - 1)
            second_product(pair)
        corrector(pair_d)
